import numpy as np
import ml_dtypes


def mxq(x, axis, fmt="e4m3"):
    dtype, down = {"e4m3": (ml_dtypes.float8_e4m3fn, 7), "e5m2": (ml_dtypes.float8_e5m2, 14)}[fmt]
    v = np.moveaxis(np.asarray(x, np.float32).astype(ml_dtypes.bfloat16).astype(np.float64), axis, -1)
    blocks = v.reshape(v.shape[:-1] + (-1, 32))
    amax = np.abs(blocks).max(-1, keepdims=True)
    byte = np.maximum(np.where(amax > 0, np.frexp(amax)[1] - 1 + 127, 0) - down, 1)
    scale = np.exp2(byte - 127.0)
    codes = (blocks / scale).astype(np.float32).astype(dtype).astype(np.float64)
    return np.moveaxis((codes * scale).reshape(v.shape), -1, axis)


WIDE = False


def mx_kscale(k):
    if not WIDE:
        return np.ones(k)
    levels = np.array([20, -20, 10, -10, 0])
    a = np.random.permutation(np.resize(levels, k // 512 * 4)).reshape(k // 512, 4)
    idx = np.arange(k)
    return np.exp2(a[idx // 512, idx % 128 // 32])


BF16 = ml_dtypes.bfloat16


def bf(x):
    return np.asarray(x, np.float32).astype(BF16)


def f64(x):
    return np.asarray(x).astype(np.float64)


B, T, D, H = 4, 256, 1024, 4096
N = B * T


def _grid(rows, cols):
    n = np.random.randint(-127, 128, (rows, cols)) * 1.0
    n[np.arange(rows), np.random.randint(0, cols, rows)] = 127.0
    return n


def setup_inputs():
    s = mx_kscale(N)[:, None]
    x = _grid(N, D) * 2.0 ** -6 * s
    w = _grid(H, D).T * 2.0 ** -12
    g = np.random.standard_normal((N, H)) * np.exp2(np.random.randint(-12, 1, (N, 1))) / s
    return {"inputs": bf(x.reshape(B, T, D)), "kernel": bf(w), "grad_out": bf(g.reshape(B, T, H))}


def reference(inputs, kernel, grad_out):
    x = f64(inputs).reshape(N, D)
    g = f64(grad_out).reshape(N, H)
    return mxq(x, 0, "e4m3").T @ mxq(g, 0, "e5m2")

@@ -1,0 +1,144 @@
+from contextlib import ExitStack
+
+import concourse.mybir as mybir
+
+BF16 = mybir.dt.bfloat16
+F32 = mybir.dt.float32
+U32 = mybir.dt.uint32
+U8 = mybir.dt.uint8
+FORMAT = {"x": mybir.dt.float8_e4m3fn_x4, "g": mybir.dt.float8_e5m2_x4}
+
+TOKENS, D, H = 1024, 1024, 4096
+FLOPS = 2 * TOKENS * D * H
+BYTES = 2 * TOKENS * (D + H) + 4 * D * H
+
+P = 128
+PACK = 4
+K_PASS = P * PACK
+PASSES = TOKENS // K_PASS
+UNIT = 512
+STORE = 2048
+RUN = 4
+
+LOADS = [
+    ("g", 0, 0, 1024),
+    ("x", 0, 0, 1024),
+    ("x", 1, 0, 1024),
+    ("g", 1, 0, 1024),
+    ("g", 0, 1024, 2048),
+    ("g", 1, 1024, 2048),
+    ("g", 0, 2048, 4096),
+    ("g", 1, 2048, 4096),
+]
+SHARED_LOADS = 6
+
+
+def tile_densegeneral_kernel(tc, inputs, kernel, grad_out, out):
+    nc = tc.nc
+    dram = {"x": inputs.flatten_outer_dims(), "g": grad_out.flatten_outer_dims()}
+
+    with ExitStack() as ctx:
+        raw_pool = ctx.enter_context(tc.tile_pool(name="raw", bufs=1))
+        grouped_pool = ctx.enter_context(tc.tile_pool(name="grouped", bufs=5))
+        mx_pool = ctx.enter_context(tc.tile_pool(name="mx", bufs=1))
+        stage_pool = ctx.enter_context(tc.tile_pool(name="stage", bufs=10))
+        psum_pool = ctx.enter_context(tc.psum_pool(name="psum", bufs=8))
+        ctx.enter_context(tc.manual_schedule())
+
+        raw = {}
+        grouped = {}
+        codes = {}
+        scales = {}
+
+        for operand, c, lo, hi in LOADS:
+            tile = raw_pool.tile([P, PACK, hi - lo], BF16, name="raw_%s%d_%d" % (operand, c, lo))
+            rows = dram[operand][c * K_PASS : (c + 1) * K_PASS, lo:hi]
+            nc.sync.dma_start(out=tile[:], in_=rows.rearrange("(p j) w -> p j w", j=PACK))
+            for u in range(lo // UNIT, hi // UNIT):
+                raw[(operand, c, u)] = tile[:, :, u * UNIT - lo : (u + 1) * UNIT - lo]
+
+        def regroup(copy, unit):
+            tile = grouped_pool.tile([P, UNIT, PACK], BF16, name="grouped", align_bytes=64)
+            copy(
+                out=tile[:].rearrange("p (w i) j -> p w j i", i=RUN),
+                in_=raw[unit].rearrange("p j (w i) -> p w j i", i=RUN),
+            )
+            grouped[unit] = tile
+
+        def quantise(unit):
+            name = "%s%d_%d" % unit
+            codes[unit] = mx_pool.tile([P, UNIT], U32, name="codes_" + name, align_bytes=64)
+            scales[unit] = mx_pool.tile([P, UNIT], U8, name="scales_" + name, align_bytes=64)
+            nc.vector.quantize_mx(
+                out=codes[unit][:].bitcast(FORMAT[unit[0]]),
+                scales=scales[unit][:],
+                in_=grouped[unit][:].rearrange("p w j -> p (w j)"),
+            )
+
+        stage = {}
+        filled = {}
+
+        def group(d, hq, copy):
+            acc = psum_pool.tile([P, UNIT], F32, name="acc")
+            cols = slice((d % 4) * P, (d % 4 + 1) * P)
+            for c in range(PASSES):
+                xu = ("x", c, d // 4)
+                gu = ("g", c, hq)
+                nc.tensor.matmul_mx(
+                    out=acc[:],
+                    lhsT=codes[xu][:, cols].bitcast(FORMAT["x"]),
+                    lhsT_scale=scales[xu][:, cols],
+                    rhs=codes[gu][:].bitcast(FORMAT["g"]),
+                    rhs_scale=scales[gu][:],
+                    start=(c == 0),
+                    stop=(c == PASSES - 1),
+                )
+            part = (d, hq * UNIT // STORE)
+            if part not in stage:
+                stage[part] = stage_pool.tile([P, STORE], F32, name="stage")
+                filled[part] = 0
+            at = hq * UNIT % STORE
+            copy(out=stage[part][:, at : at + UNIT], in_=acc[:])
+            filled[part] += UNIT
+            if filled[part] == STORE:
+                nc.sync.dma_start(
+                    out=out[d * P : (d + 1) * P, part[1] * STORE : (part[1] + 1) * STORE], in_=stage[part][:]
+                )
+
+        vector, scalar = nc.vector.tensor_copy, nc.scalar.copy
+
+        late = None
+        for operand, c, lo, hi in LOADS[:SHARED_LOADS]:
+            a, b = (operand, c, lo // UNIT), (operand, c, lo // UNIT + 1)
+            regroup(vector, a)
+            regroup(scalar, b)
+            if late is not None:
+                quantise(late)
+            quantise(a)
+            late = b
+        quantise(late)
+
+        n = 0
+        for hq in (0, 1):
+            for d in range(4):
+                group(d, hq, vector if n in (1, 3, 5) else scalar)
+                n += 1
+
+        late = None
+        for operand, c, lo, hi in LOADS[SHARED_LOADS:]:
+            for u in range(lo // UNIT, hi // UNIT):
+                regroup(vector, (operand, c, u))
+                if late is not None:
+                    quantise(late)
+                late = (operand, c, u)
+        quantise(late)
+
+        for d in range(4):
+            for hq in (2, 3):
+                group(d, hq, scalar)
+        for d in range(4, 8):
+            for hq in range(4):
+                group(d, hq, scalar)
+        for d in range(8):
+            for hq in range(4, 8):
+                group(d, hq, vector if hq % 2 == 1 else scalar)

@@ -118,11 +118,11 @@ def tile_densegeneral_kernel(tc, inputs, kernel, grad_out, out):
             late = b
         quantise(late)
 
-        n = 0
         for hq in (0, 1):
             for d in range(4):
-                group(d, hq, vector if n in (1, 3, 5) else scalar)
-                n += 1
+                group(d, hq, vector if (d, hq) in ((1, 0), (3, 0)) else scalar)
+        for hq in (2, 3):
+            group(0, hq, vector)
 
         late = None
         for operand, c, lo, hi in LOADS[SHARED_LOADS:]:
@@ -133,7 +133,7 @@ def tile_densegeneral_kernel(tc, inputs, kernel, grad_out, out):
                 late = (operand, c, u)
         quantise(late)
 
-        for d in range(4):
+        for d in range(1, 4):
             for hq in (2, 3):
                 group(d, hq, scalar)
         for d in range(4, 8):

@@ -43,7 +43,6 @@ def tile_densegeneral_kernel(tc, inputs, kernel, grad_out, out):
         mx_pool = ctx.enter_context(tc.tile_pool(name="mx", bufs=1))
         stage_pool = ctx.enter_context(tc.tile_pool(name="stage", bufs=10))
         psum_pool = ctx.enter_context(tc.psum_pool(name="psum", bufs=8))
-        ctx.enter_context(tc.manual_schedule())
 
         raw = {}
         grouped = {}
@@ -118,11 +117,11 @@ def tile_densegeneral_kernel(tc, inputs, kernel, grad_out, out):
             late = b
         quantise(late)
 
+        n = 0
         for hq in (0, 1):
             for d in range(4):
-                group(d, hq, vector if (d, hq) in ((1, 0), (3, 0)) else scalar)
-        for hq in (2, 3):
-            group(0, hq, vector)
+                group(d, hq, vector if n in (1, 3, 5) else scalar)
+                n += 1
 
         late = None
         for operand, c, lo, hi in LOADS[SHARED_LOADS:]:
@@ -133,7 +132,7 @@ def tile_densegeneral_kernel(tc, inputs, kernel, grad_out, out):
                 late = (operand, c, u)
         quantise(late)
 
-        for d in range(1, 4):
+        for d in range(4):
             for hq in (2, 3):
                 group(d, hq, scalar)
         for d in range(4, 8):

@@ -21,16 +21,14 @@ STORE = 2048
 RUN = 4
 
 LOADS = [
-    ("g", 0, 0, 1024),
     ("x", 0, 0, 1024),
     ("x", 1, 0, 1024),
-    ("g", 1, 0, 1024),
-    ("g", 0, 1024, 2048),
-    ("g", 1, 1024, 2048),
+    ("g", 0, 0, 2048),
+    ("g", 1, 0, 2048),
     ("g", 0, 2048, 4096),
     ("g", 1, 2048, 4096),
 ]
-SHARED_LOADS = 6
+SHARED_LOADS = 4
 
 
 def tile_densegeneral_kernel(tc, inputs, kernel, grad_out, out):
@@ -43,6 +41,7 @@ def tile_densegeneral_kernel(tc, inputs, kernel, grad_out, out):
         mx_pool = ctx.enter_context(tc.tile_pool(name="mx", bufs=1))
         stage_pool = ctx.enter_context(tc.tile_pool(name="stage", bufs=10))
         psum_pool = ctx.enter_context(tc.psum_pool(name="psum", bufs=8))
+        ctx.enter_context(tc.manual_schedule())
 
         raw = {}
         grouped = {}
@@ -74,54 +73,65 @@ def tile_densegeneral_kernel(tc, inputs, kernel, grad_out, out):
                 in_=grouped[unit][:].rearrange("p w j -> p (w j)"),
             )
 
+        acc = {}
         stage = {}
         filled = {}
 
-        def group(d, hq, copy):
-            acc = psum_pool.tile([P, UNIT], F32, name="acc")
+        def mx_pass(d, hq, c):
+            if c == 0:
+                acc[(d, hq)] = psum_pool.tile([P, UNIT], F32, name="acc")
             cols = slice((d % 4) * P, (d % 4 + 1) * P)
-            for c in range(PASSES):
-                xu = ("x", c, d // 4)
-                gu = ("g", c, hq)
-                nc.tensor.matmul_mx(
-                    out=acc[:],
-                    lhsT=codes[xu][:, cols].bitcast(FORMAT["x"]),
-                    lhsT_scale=scales[xu][:, cols],
-                    rhs=codes[gu][:].bitcast(FORMAT["g"]),
-                    rhs_scale=scales[gu][:],
-                    start=(c == 0),
-                    stop=(c == PASSES - 1),
-                )
+            xu = ("x", c, d // 4)
+            gu = ("g", c, hq)
+            nc.tensor.matmul_mx(
+                out=acc[(d, hq)][:],
+                lhsT=codes[xu][:, cols].bitcast(FORMAT["x"]),
+                lhsT_scale=scales[xu][:, cols],
+                rhs=codes[gu][:].bitcast(FORMAT["g"]),
+                rhs_scale=scales[gu][:],
+                start=(c == 0),
+                stop=(c == PASSES - 1),
+            )
+
+        def empty(d, hq, copy):
             part = (d, hq * UNIT // STORE)
             if part not in stage:
                 stage[part] = stage_pool.tile([P, STORE], F32, name="stage")
                 filled[part] = 0
             at = hq * UNIT % STORE
-            copy(out=stage[part][:, at : at + UNIT], in_=acc[:])
+            copy(out=stage[part][:, at : at + UNIT], in_=acc[(d, hq)][:])
             filled[part] += UNIT
             if filled[part] == STORE:
                 nc.sync.dma_start(
                     out=out[d * P : (d + 1) * P, part[1] * STORE : (part[1] + 1) * STORE], in_=stage[part][:]
                 )
 
+        def group(d, hq, copy):
+            for c in range(PASSES):
+                mx_pass(d, hq, c)
+            empty(d, hq, copy)
+
         vector, scalar = nc.vector.tensor_copy, nc.scalar.copy
 
         late = None
         for operand, c, lo, hi in LOADS[:SHARED_LOADS]:
-            a, b = (operand, c, lo // UNIT), (operand, c, lo // UNIT + 1)
-            regroup(vector, a)
-            regroup(scalar, b)
-            if late is not None:
-                quantise(late)
-            quantise(a)
-            late = b
+            for u in range(lo // UNIT, hi // UNIT, 2):
+                a, b = (operand, c, u), (operand, c, u + 1)
+                regroup(vector, a)
+                regroup(scalar, b)
+                if late is not None:
+                    quantise(late)
+                quantise(a)
+                late = b
         quantise(late)
 
-        n = 0
-        for hq in (0, 1):
-            for d in range(4):
-                group(d, hq, vector if n in (1, 3, 5) else scalar)
-                n += 1
+        for c in range(PASSES):
+            for hq in range(4):
+                for d in range(2):
+                    mx_pass(d, hq, c)
+        for d in range(2):
+            for hq in range(4):
+                empty(d, hq, scalar if hq < 2 else vector)
 
         late = None
         for operand, c, lo, hi in LOADS[SHARED_LOADS:]:
@@ -132,10 +142,7 @@ def tile_densegeneral_kernel(tc, inputs, kernel, grad_out, out):
                 late = (operand, c, u)
         quantise(late)
 
-        for d in range(4):
-            for hq in (2, 3):
-                group(d, hq, scalar)
-        for d in range(4, 8):
+        for d in range(2, 8):
             for hq in range(4):
                 group(d, hq, scalar)
         for d in range(8):

from contextlib import ExitStack

import concourse.mybir as mybir

BF16 = mybir.dt.bfloat16
F32 = mybir.dt.float32
U32 = mybir.dt.uint32
U8 = mybir.dt.uint8
FORMAT = {"x": mybir.dt.float8_e4m3fn_x4, "g": mybir.dt.float8_e5m2_x4}

TOKENS, D, H = 1024, 1024, 4096
FLOPS = 2 * TOKENS * D * H
BYTES = 2 * TOKENS * (D + H) + 4 * D * H

P = 128
PACK = 4
K_PASS = P * PACK
PASSES = TOKENS // K_PASS
UNIT = 512
STORE = 2048
RUN = 4

LOADS = [
    ("x", 0, 0, 1024),
    ("x", 1, 0, 1024),
    ("g", 0, 0, 2048),
    ("g", 1, 0, 2048),
    ("g", 0, 2048, 4096),
    ("g", 1, 2048, 4096),
]
SHARED_LOADS = 4


def tile_densegeneral_kernel(tc, inputs, kernel, grad_out, out):
    nc = tc.nc
    dram = {"x": inputs.flatten_outer_dims(), "g": grad_out.flatten_outer_dims()}

    with ExitStack() as ctx:
        raw_pool = ctx.enter_context(tc.tile_pool(name="raw", bufs=1))
        grouped_pool = ctx.enter_context(tc.tile_pool(name="grouped", bufs=5))
        mx_pool = ctx.enter_context(tc.tile_pool(name="mx", bufs=1))
        stage_pool = ctx.enter_context(tc.tile_pool(name="stage", bufs=10))
        psum_pool = ctx.enter_context(tc.psum_pool(name="psum", bufs=8))
        ctx.enter_context(tc.manual_schedule())

        raw = {}
        grouped = {}
        codes = {}
        scales = {}

        for operand, c, lo, hi in LOADS:
            tile = raw_pool.tile([P, PACK, hi - lo], BF16, name="raw_%s%d_%d" % (operand, c, lo))
            rows = dram[operand][c * K_PASS : (c + 1) * K_PASS, lo:hi]
            nc.sync.dma_start(out=tile[:], in_=rows.rearrange("(p j) w -> p j w", j=PACK))
            for u in range(lo // UNIT, hi // UNIT):
                raw[(operand, c, u)] = tile[:, :, u * UNIT - lo : (u + 1) * UNIT - lo]

        def regroup(copy, unit):
            tile = grouped_pool.tile([P, UNIT, PACK], BF16, name="grouped", align_bytes=64)
            copy(
                out=tile[:].rearrange("p (w i) j -> p w j i", i=RUN),
                in_=raw[unit].rearrange("p j (w i) -> p w j i", i=RUN),
            )
            grouped[unit] = tile

        def quantise(unit):
            name = "%s%d_%d" % unit
            codes[unit] = mx_pool.tile([P, UNIT], U32, name="codes_" + name, align_bytes=64)
            scales[unit] = mx_pool.tile([P, UNIT], U8, name="scales_" + name, align_bytes=64)
            nc.vector.quantize_mx(
                out=codes[unit][:].bitcast(FORMAT[unit[0]]),
                scales=scales[unit][:],
                in_=grouped[unit][:].rearrange("p w j -> p (w j)"),
            )

        acc = {}
        stage = {}
        filled = {}

        def mx_pass(d, hq, c):
            if c == 0:
                acc[(d, hq)] = psum_pool.tile([P, UNIT], F32, name="acc")
            cols = slice((d % 4) * P, (d % 4 + 1) * P)
            xu = ("x", c, d // 4)
            gu = ("g", c, hq)
            nc.tensor.matmul_mx(
                out=acc[(d, hq)][:],
                lhsT=codes[xu][:, cols].bitcast(FORMAT["x"]),
                lhsT_scale=scales[xu][:, cols],
                rhs=codes[gu][:].bitcast(FORMAT["g"]),
                rhs_scale=scales[gu][:],
                start=(c == 0),
                stop=(c == PASSES - 1),
            )

        def empty(d, hq, copy):
            part = (d, hq * UNIT // STORE)
            if part not in stage:
                stage[part] = stage_pool.tile([P, STORE], F32, name="stage")
                filled[part] = 0
            at = hq * UNIT % STORE
            copy(out=stage[part][:, at : at + UNIT], in_=acc[(d, hq)][:])
            filled[part] += UNIT
            if filled[part] == STORE:
                nc.sync.dma_start(
                    out=out[d * P : (d + 1) * P, part[1] * STORE : (part[1] + 1) * STORE], in_=stage[part][:]
                )

        def group(d, hq, copy):
            for c in range(PASSES):
                mx_pass(d, hq, c)
            empty(d, hq, copy)

        vector, scalar = nc.vector.tensor_copy, nc.scalar.copy

        late = None
        for operand, c, lo, hi in LOADS[:SHARED_LOADS]:
            for u in range(lo // UNIT, hi // UNIT, 2):
                a, b = (operand, c, u), (operand, c, u + 1)
                regroup(vector, a)
                regroup(scalar, b)
                if late is not None:
                    quantise(late)
                quantise(a)
                late = b
        quantise(late)

        for c in range(PASSES):
            for hq in range(4):
                for d in range(2):
                    mx_pass(d, hq, c)
        for d in range(2):
            for hq in range(4):
                empty(d, hq, scalar if hq < 2 else vector)

        late = None
        for operand, c, lo, hi in LOADS[SHARED_LOADS:]:
            for u in range(lo // UNIT, hi // UNIT):
                regroup(vector, (operand, c, u))
                if late is not None:
                    quantise(late)
                late = (operand, c, u)
        quantise(late)

        for d in range(2, 8):
            for hq in range(4):
                group(d, hq, scalar)
        for d in range(8):
            for hq in range(4, 8):
                group(d, hq, vector if hq % 2 == 1 else scalar)
